import numpy as np
import ml_dtypes


def mxq(x, axis, fmt="e4m3"):
    dtype, down = {"e4m3": (ml_dtypes.float8_e4m3fn, 7), "e5m2": (ml_dtypes.float8_e5m2, 14)}[fmt]
    v = np.moveaxis(np.asarray(x, np.float32).astype(ml_dtypes.bfloat16).astype(np.float64), axis, -1)
    blocks = v.reshape(v.shape[:-1] + (-1, 32))
    amax = np.abs(blocks).max(-1, keepdims=True)
    byte = np.maximum(np.where(amax > 0, np.frexp(amax)[1] - 1 + 127, 0) - down, 1)
    scale = np.exp2(byte - 127.0)
    codes = (blocks / scale).astype(np.float32).astype(dtype).astype(np.float64)
    return np.moveaxis((codes * scale).reshape(v.shape), -1, axis)


WIDE = False


def mx_kscale(k):
    if not WIDE:
        return np.ones(k)
    levels = np.array([10, -10, 5, -5, 0])
    a = np.random.permutation(np.resize(levels, k // 512 * 4)).reshape(k // 512, 4)
    idx = np.arange(k)
    return np.exp2(a[idx // 512, idx % 128 // 32])


BF16 = ml_dtypes.bfloat16


def bf(x):
    return np.asarray(x, np.float32).astype(BF16)


def f64(x):
    return np.asarray(x).astype(np.float64)


E2M1 = np.array([0.0, 0.5, 1.0, 1.5, 2.0, 3.0, 4.0, 6.0, -0.0, -0.5, -1.0, -1.5, -2.0, -3.0, -4.0, -6.0])


def pack_weight(w, fmt):
    k, n = w.shape
    w = f64(bf(w)).reshape(k // 32, 32, n)
    amax = np.abs(w).max(1)
    if fmt == "e4m3":
        byte = np.frexp(amax)[1] - 1 + 127 - 7
    else:
        mant, ex = np.frexp(amax / 6.0)
        byte = np.where(mant > 0.5, ex, ex - 1) + 127
    byte = np.clip(np.where(amax > 0, byte, 1), 1, 254)
    scaled = (w * np.exp2(127.0 - byte)[:, None, :]).reshape(k, n).astype(np.float32)
    by_word = np.ascontiguousarray(scaled.reshape(k // 512, 128, 4, n).transpose(0, 1, 3, 2))
    if fmt == "e4m3":
        words = by_word.astype(ml_dtypes.float8_e4m3fn).view(np.uint8)
    else:
        c = by_word.astype(ml_dtypes.float4_e2m1fn).view(np.uint8) & 0xF
        words = c[..., 0::2] | (c[..., 1::2] << 4)
    return np.ascontiguousarray(words), np.ascontiguousarray(byte.astype(np.uint8).reshape(k // 512, 16, n))


def unpack_weight(words, scales, fmt):
    g, p, n, _ = words.shape
    if fmt == "e4m3":
        vals = np.ascontiguousarray(words).view(ml_dtypes.float8_e4m3fn).astype(np.float64)
    else:
        nib = np.empty((g, p, n, 4), np.uint8)
        nib[..., 0::2] = words & 0xF
        nib[..., 1::2] = words >> 4
        vals = E2M1[nib]
    vals = vals * np.repeat(np.exp2(scales.astype(np.float64) - 127.0), 8, axis=1)[..., None]
    return vals.transpose(0, 1, 3, 2).reshape(g * 512, n)


B, IN, H = 128, 2048, 2048
QH = H % (16 * 32) == 0
FMT = "e4m3"


def sigmoid(v):
    return 1.0 / (1.0 + np.exp(-v))


def setup_inputs():
    s = mx_kscale(IN)
    one = np.ones(H)
    inp = {"x": bf(np.random.standard_normal((B, IN)) * s), "hidden": bf(np.random.standard_normal((B, H)))}
    for name, fan_in, f in (("Wir", IN, s), ("Whr", H, one), ("Wiz", IN, s), ("Whz", H, one), ("Win", IN, s), ("Whn", H, one)):
        w = np.random.standard_normal((H, fan_in)) / np.sqrt(fan_in) / f[None, :]
        words, scales = pack_weight(np.ascontiguousarray(w.T), FMT)
        inp[name + "_w_words"] = words
        inp[name + "_w_scales"] = scales
        inp[name + "_b"] = bf(np.random.standard_normal(H) * 0.2)
    return inp


def reference(x, hidden, Wir_w_words, Wir_w_scales, Wir_b, Whr_w_words, Whr_w_scales, Whr_b, Wiz_w_words, Wiz_w_scales, Wiz_b, Whz_w_words, Whz_w_scales, Whz_b, Win_w_words, Win_w_scales, Win_b, Whn_w_words, Whn_w_scales, Whn_b):
    x, hidden = f64(x), f64(hidden)
    Wi = np.concatenate([unpack_weight(Wir_w_words, Wir_w_scales, FMT).T, unpack_weight(Wiz_w_words, Wiz_w_scales, FMT).T, unpack_weight(Win_w_words, Win_w_scales, FMT).T], axis=0)
    Wh = np.concatenate([unpack_weight(Whr_w_words, Whr_w_scales, FMT).T, unpack_weight(Whz_w_words, Whz_w_scales, FMT).T, unpack_weight(Whn_w_words, Whn_w_scales, FMT).T], axis=0)
    bi = np.concatenate([f64(Wir_b), f64(Wiz_b), f64(Win_b)], axis=0)
    bh = np.concatenate([f64(Whr_b), f64(Whz_b), f64(Whn_b)], axis=0)
    gi = (mxq(x, 1, "e4m3") @ Wi.T) + bi
    if QH:
        gh = (mxq(hidden, 1, "e4m3") @ Wh.T) + bh
    else:
        gh = hidden @ Wh.T + bh
    ir, iz, inn = np.split(gi, 3, axis=1)
    hr, hz, hn = np.split(gh, 3, axis=1)
    rt = sigmoid(ir + hr)
    zt = sigmoid(iz + hz)
    nt = np.tanh(inn + rt * hn)
    ht = (1.0 - zt) * nt + zt * hidden
    return ht

@@ -1,0 +1,206 @@
+from contextlib import ExitStack
+
+import concourse.mybir as mybir
+from concourse.masks import make_identity
+
+F32 = mybir.dt.float32
+BF16 = mybir.dt.bfloat16
+I32 = mybir.dt.int32
+U32 = mybir.dt.uint32
+U8 = mybir.dt.uint8
+FP8X4 = mybir.dt.float8_e4m3fn_x4
+ADD = mybir.AluOpType.add
+SUB = mybir.AluOpType.subtract
+MUL = mybir.AluOpType.mult
+ACT = mybir.ActivationFunctionType
+
+P = 128
+H = 2048
+G = 4
+NT = 512
+FLOPS = 2 * 128 * 2048 * 2048 * 6
+
+NW = 12
+SCALE_MODE = "woven"
+ZCH = ((0, 512), (512, 512), (1024, 512), (1536, 256), (1792, 128), (1920, 128))
+ZBANK = (4, 5, 6, 7, 0, 1, 2, 3)
+
+
+def tile_gru_w_kernel(
+    tc, x, hidden,
+    Wir_w, Wir_s, Wir_b, Whr_w, Whr_s, Whr_b,
+    Wiz_w, Wiz_s, Wiz_b, Whz_w, Whz_s, Whz_b,
+    Win_w, Win_s, Win_b, Whn_w, Whn_s, Whn_b,
+    out,
+):
+    nc = tc.nc
+    with ExitStack() as ctx:
+        keep = ctx.enter_context(tc.tile_pool(name="keep", bufs=1))
+        wpool = ctx.enter_context(tc.tile_pool(name="wpool", bufs=NW))
+        psum = ctx.enter_context(tc.psum_pool(name="psum", bufs=1))
+
+        def bank(i, shape):
+            return psum.tile(shape, F32, name="bk%d" % i, tag="bk%d" % i)
+
+        def cols(j):
+            return slice(NT * j, NT * (j + 1))
+
+        order = (("ir", Wir_s), ("hr", Whr_s), ("hn", Whn_s), ("in", Win_s), ("iz", Wiz_s), ("hz", Whz_s))
+        planes = {}
+        for nm, s in order:
+            pl = keep.tile([P, H], U8, name="pl_" + nm, align_bytes=64)
+            nc.vector.memset(pl[:].bitcast(I32), 0)
+            planes[nm] = pl
+        brow = keep.tile([P, H], BF16, name="brow")
+        nc.vector.memset(brow[:].bitcast(I32), 0)
+        sel = keep.tile([P, 4, P], BF16, name="sel")
+        nc.vector.memset(sel[:].rearrange("p q m -> p (q m)").bitcast(I32), 0)
+        for q in range(4):
+            nc.vector.memset(sel[32 * q:32 * q + 32, q, :], 1.0)
+        warm = keep.tile([P, 2], F32, name="warm")
+        nc.vector.memset(warm[:], 0.0)
+        nc.scalar.activation(out=warm[:, 1:2], in_=warm[:, 0:1], func=ACT.Sigmoid)
+        ident = keep.tile([P, P], F32, name="ident")
+        make_identity(nc, ident[:])
+
+        x_sb = keep.tile([P, H], BF16, name="x_sb")
+        h_sb = keep.tile([P, H], BF16, name="h_sb")
+        nc.sync.dma_start(out=x_sb[:], in_=x)
+        nc.sync.dma_start(out=h_sb[:], in_=hidden)
+
+        def load_scales(nm, s):
+            pl = planes[nm]
+            for q in (0, 2, 1, 3):
+                if SCALE_MODE == "gpsimd" and nm != "ir":
+                    nc.gpsimd.dma_start(out=pl[32 * q:32 * q + 16, :].bitcast(F32), in_=s[:, 4 * q:4 * q + 4, :].bitcast(F32))
+                else:
+                    nc.sync.dma_start(out=pl[32 * q:32 * q + 16, :].bitcast(I32), in_=s[:, 4 * q:4 * q + 4, :].bitcast(I32))
+
+        def load_bias(row, b):
+            nc.gpsimd.dma_start(out=brow[row:row + 1, :], in_=b.unsqueeze(0))
+
+        if SCALE_MODE == "front":
+            for nm, s in order:
+                load_scales(nm, s)
+        if SCALE_MODE == "gpsimd":
+            load_scales("ir", Wir_s)
+            load_scales("hr", Whr_s)
+        load_bias(0, Wir_b)
+        load_bias(1, Whr_b)
+        if SCALE_MODE == "gpsimd":
+            load_scales("hn", Whn_s)
+        load_bias(32, Whn_b)
+        load_bias(64, Win_b)
+        if SCALE_MODE == "gpsimd":
+            load_scales("in", Win_s)
+            load_scales("iz", Wiz_s)
+        load_bias(96, Wiz_b)
+        load_bias(97, Whz_b)
+        if SCALE_MODE == "gpsimd":
+            load_scales("hz", Whz_s)
+
+        def load_full(nm, s, words, g):
+            if g == 0 and SCALE_MODE == "woven":
+                load_scales(nm, s)
+            w = wpool.tile([P, H], U32, name="w", tag="w", align_bytes=64)
+            nc.sync.dma_start(out=w[:].bitcast(I32), in_=words[g].rearrange("p n t -> p (n t)").bitcast(I32))
+            return w
+
+        def quantise(src, nm, banks, copy):
+            words = src[:].bitcast(F32)
+            grouped = keep.tile([P, H], BF16, name="grp_" + nm, align_bytes=64)
+            codes = keep.tile([P, G * P], U32, name="cod_" + nm, align_bytes=64)
+            scl = keep.tile([P, G * P], U8, name="scl_" + nm, align_bytes=64)
+            gview = grouped[:].bitcast(F32).rearrange("p (g b u) -> p g b u", g=G, u=2)
+            for half in range(2):
+                xt = bank(banks[half], [P, 4, P])
+                for gl in range(2):
+                    g = 2 * half + gl
+                    for u in range(2):
+                        nc.tensor.transpose(xt[:, 2 * gl + u, :], words[:, 256 * g + u:256 * (g + 1):2], ident[:])
+                copy(out=gview[:, 2 * half:2 * half + 2, :, :], in_=xt[:].rearrange("p (gl u) b -> p gl b u", u=2))
+            return grouped, codes, scl
+
+        xg, xc, xs = quantise(x_sb, "x", (0, 1), nc.vector.tensor_copy)
+        hg, hc, hs = quantise(h_sb, "h", (2, 3), nc.scalar.copy)
+        nc.vector.quantize_mx(out=xc[:].bitcast(FP8X4), scales=xs[:], in_=xg[:])
+        nc.vector.quantize_mx(out=hc[:].bitcast(FP8X4), scales=hs[:], in_=hg[:])
+
+        bias = {}
+        for q, nm in ((0, "r"), (1, "hn"), (2, "in"), (3, "z")):
+            bt = keep.tile([P, H], F32, name="bias_" + nm)
+            for j in range(4):
+                pb = bank(4 + j, [P, NT])
+                nc.tensor.matmul(pb[:], lhsT=sel[:, q, :], rhs=brow[:, cols(j)], start=True, stop=True)
+                if j % 2 == 0:
+                    nc.scalar.copy(out=bt[:, cols(j)], in_=pb[:])
+                else:
+                    nc.vector.tensor_copy(out=bt[:, cols(j)], in_=pb[:])
+            bias[nm] = bt
+
+        def mx(acc, cd, sc, g, w_ap, s_ap, start, stop):
+            nc.tensor.matmul_mx(
+                out=acc,
+                lhsT=cd[:, P * g:P * (g + 1)].bitcast(FP8X4),
+                lhsT_scale=sc[:, P * g:P * (g + 1)],
+                rhs=w_ap.bitcast(FP8X4),
+                rhs_scale=s_ap,
+                start=start,
+                stop=stop,
+            )
+
+        def full_phase(accs, parts):
+            n = len(parts)
+            for i, (nm, s, words, cd, sc) in enumerate(parts):
+                for g in range(G):
+                    w = load_full(nm, s, words, g)
+                    for j in range(4):
+                        mx(accs[j][:], cd, sc, g, w[:, cols(j)], planes[nm][4 * g:P, cols(j)],
+                           i == 0 and g == 0, i == n - 1 and g == G - 1)
+
+        r_t = keep.tile([P, H], F32, name="r_t")
+        acc = [bank(j, [P, NT]) for j in range(4)]
+        full_phase(acc, (("ir", Wir_s, Wir_w, xc, xs), ("hr", Whr_s, Whr_w, hc, hs)))
+        for j in range(4):
+            nc.vector.tensor_tensor(out=r_t[:, cols(j)], in0=acc[j][:], in1=bias["r"][:, cols(j)], op=ADD)
+            nc.scalar.activation(out=r_t[:, cols(j)], in_=r_t[:, cols(j)], func=ACT.Sigmoid)
+
+        c_t = keep.tile([P, H], F32, name="c_t")
+        acc = [bank(4 + j, [P, NT]) for j in range(4)]
+        full_phase(acc, (("hn", Whn_s, Whn_w, hc, hs),))
+        for j in range(4):
+            cs = cols(j)
+            nc.vector.tensor_tensor(out=c_t[:, cs], in0=acc[j][:], in1=bias["hn"][:, cs], op=ADD)
+            nc.vector.tensor_tensor(out=c_t[:, cs], in0=c_t[:, cs], in1=r_t[:, cs], op=MUL)
+            nc.vector.tensor_tensor(out=c_t[:, cs], in0=c_t[:, cs], in1=bias["in"][:, cs], op=ADD)
+
+        n_t = keep.tile([P, H], F32, name="n_t")
+        d_t = keep.tile([P, H], F32, name="d_t")
+        acc = [bank(j, [P, NT]) for j in range(4)]
+        full_phase(acc, (("in", Win_s, Win_w, xc, xs),))
+        for j in range(4):
+            cs = cols(j)
+            nc.vector.tensor_tensor(out=n_t[:, cs], in0=acc[j][:], in1=c_t[:, cs], op=ADD)
+            nc.scalar.activation(out=n_t[:, cs], in_=n_t[:, cs], func=ACT.Tanh)
+            nc.vector.tensor_tensor(out=d_t[:, cs], in0=h_sb[:, cs], in1=n_t[:, cs], op=SUB)
+
+        z_t = keep.tile([P, H], F32, name="z_t")
+        accz = [bank(ZBANK[c], [P, wd]) for c, (c0, wd) in enumerate(ZCH)]
+        for g in range(G):
+            w = load_full("iz", Wiz_s, Wiz_w, g)
+            for c, (c0, wd) in enumerate(ZCH):
+                mx(accz[c][:], xc, xs, g, w[:, c0:c0 + wd], planes["iz"][4 * g:P, c0:c0 + wd], g == 0, False)
+        if SCALE_MODE == "woven":
+            load_scales("hz", Whz_s)
+        for c, (c0, wd) in enumerate(ZCH):
+            cs = slice(c0, c0 + wd)
+            wz = wpool.tile([P, G, wd], U32, name="w", tag="w", align_bytes=64)
+            nc.sync.dma_start(out=wz[:].bitcast(I32),
+                              in_=Whz_w[:, :, cs, :].rearrange("g p n t -> p g (n t)").bitcast(I32))
+            for g in range(G):
+                mx(accz[c][:], hc, hs, g, wz[:, g, :], planes["hz"][4 * g:P, cs], False, g == G - 1)
+            nc.vector.tensor_tensor(out=z_t[:, cs], in0=accz[c][:], in1=bias["z"][:, cs], op=ADD)
+            nc.scalar.activation(out=z_t[:, cs], in_=z_t[:, cs], func=ACT.Sigmoid)
+            nc.vector.tensor_tensor(out=z_t[:, cs], in0=z_t[:, cs], in1=d_t[:, cs], op=MUL)
+            nc.vector.tensor_tensor(out=z_t[:, cs], in0=z_t[:, cs], in1=n_t[:, cs], op=ADD)
+            nc.sync.dma_start(out=out[:, cs], in_=z_t[:, cs])

@@ -21,7 +21,7 @@ NT = 512
 FLOPS = 2 * 128 * 2048 * 2048 * 6
 
 NW = 12
-SCALE_MODE = "woven"
+SCALE_MODE = "gpsimd"
 ZCH = ((0, 512), (512, 512), (1024, 512), (1536, 256), (1792, 128), (1920, 128))
 ZBANK = (4, 5, 6, 7, 0, 1, 2, 3)
 

@@ -20,10 +20,9 @@ G = 4
 NT = 512
 FLOPS = 2 * 128 * 2048 * 2048 * 6
 
-NW = 12
-SCALE_MODE = "gpsimd"
+NW = 14
 ZCH = ((0, 512), (512, 512), (1024, 512), (1536, 256), (1792, 128), (1920, 128))
-ZBANK = (4, 5, 6, 7, 0, 1, 2, 3)
+ZBANK = (4, 5, 6, 7, 0, 1)
 
 
 def tile_gru_w_kernel(
@@ -38,6 +37,7 @@ def tile_gru_w_kernel(
         keep = ctx.enter_context(tc.tile_pool(name="keep", bufs=1))
         wpool = ctx.enter_context(tc.tile_pool(name="wpool", bufs=NW))
         psum = ctx.enter_context(tc.psum_pool(name="psum", bufs=1))
+        ctx.enter_context(tc.manual_schedule())
 
         def bank(i, shape):
             return psum.tile(shape, F32, name="bk%d" % i, tag="bk%d" % i)
@@ -45,66 +45,43 @@ def tile_gru_w_kernel(
         def cols(j):
             return slice(NT * j, NT * (j + 1))
 
-        order = (("ir", Wir_s), ("hr", Whr_s), ("hn", Whn_s), ("in", Win_s), ("iz", Wiz_s), ("hz", Whz_s))
+        x_sb = keep.tile([P, H], BF16, name="x_sb")
+        h_sb = keep.tile([P, H], BF16, name="h_sb")
+        nc.sync.dma_start(out=x_sb[:], in_=x)
+        nc.sync.dma_start(out=h_sb[:], in_=hidden)
+
+        ident = keep.tile([P, P], F32, name="ident")
+        make_identity(nc, ident[:])
+        warm = keep.tile([P, 2], F32, name="warm")
         planes = {}
-        for nm, s in order:
-            pl = keep.tile([P, H], U8, name="pl_" + nm, align_bytes=64)
-            nc.vector.memset(pl[:].bitcast(I32), 0)
-            planes[nm] = pl
+        for nm in ("ir", "hr"):
+            planes[nm] = keep.tile([P, H], U8, name="pl_" + nm, align_bytes=64)
+            nc.vector.memset(planes[nm][:].bitcast(I32), 0)
+        nc.vector.memset(warm[:], 0.0)
+        nc.scalar.activation(out=warm[:, 1:2], in_=warm[:, 0:1], func=ACT.Sigmoid)
         brow = keep.tile([P, H], BF16, name="brow")
         nc.vector.memset(brow[:].bitcast(I32), 0)
         sel = keep.tile([P, 4, P], BF16, name="sel")
         nc.vector.memset(sel[:].rearrange("p q m -> p (q m)").bitcast(I32), 0)
         for q in range(4):
             nc.vector.memset(sel[32 * q:32 * q + 32, q, :], 1.0)
-        warm = keep.tile([P, 2], F32, name="warm")
-        nc.vector.memset(warm[:], 0.0)
-        nc.scalar.activation(out=warm[:, 1:2], in_=warm[:, 0:1], func=ACT.Sigmoid)
-        ident = keep.tile([P, P], F32, name="ident")
-        make_identity(nc, ident[:])
-
-        x_sb = keep.tile([P, H], BF16, name="x_sb")
-        h_sb = keep.tile([P, H], BF16, name="h_sb")
-        nc.sync.dma_start(out=x_sb[:], in_=x)
-        nc.sync.dma_start(out=h_sb[:], in_=hidden)
+        for nm in ("hn", "in", "iz", "hz"):
+            planes[nm] = keep.tile([P, H], U8, name="pl_" + nm, align_bytes=64)
+            nc.vector.memset(planes[nm][:].bitcast(I32), 0)
 
         def load_scales(nm, s):
-            pl = planes[nm]
-            for q in (0, 2, 1, 3):
-                if SCALE_MODE == "gpsimd" and nm != "ir":
-                    nc.gpsimd.dma_start(out=pl[32 * q:32 * q + 16, :].bitcast(F32), in_=s[:, 4 * q:4 * q + 4, :].bitcast(F32))
-                else:
-                    nc.sync.dma_start(out=pl[32 * q:32 * q + 16, :].bitcast(I32), in_=s[:, 4 * q:4 * q + 4, :].bitcast(I32))
+            for q in range(4):
+                nc.gpsimd.dma_start(out=planes[nm][32 * q:32 * q + 16, :].bitcast(F32),
+                                    in_=s[:, 4 * q:4 * q + 4, :].bitcast(F32))
 
-        def load_bias(row, b):
+        load_scales("ir", Wir_s)
+        load_scales("hr", Whr_s)
+        for row, b in ((0, Wir_b), (1, Whr_b), (32, Whn_b), (64, Win_b), (96, Wiz_b), (97, Whz_b)):
             nc.gpsimd.dma_start(out=brow[row:row + 1, :], in_=b.unsqueeze(0))
-
-        if SCALE_MODE == "front":
-            for nm, s in order:
-                load_scales(nm, s)
-        if SCALE_MODE == "gpsimd":
-            load_scales("ir", Wir_s)
-            load_scales("hr", Whr_s)
-        load_bias(0, Wir_b)
-        load_bias(1, Whr_b)
-        if SCALE_MODE == "gpsimd":
-            load_scales("hn", Whn_s)
-        load_bias(32, Whn_b)
-        load_bias(64, Win_b)
-        if SCALE_MODE == "gpsimd":
-            load_scales("in", Win_s)
-            load_scales("iz", Wiz_s)
-        load_bias(96, Wiz_b)
-        load_bias(97, Whz_b)
-        if SCALE_MODE == "gpsimd":
-            load_scales("hz", Whz_s)
-
-        def load_full(nm, s, words, g):
-            if g == 0 and SCALE_MODE == "woven":
-                load_scales(nm, s)
-            w = wpool.tile([P, H], U32, name="w", tag="w", align_bytes=64)
-            nc.sync.dma_start(out=w[:].bitcast(I32), in_=words[g].rearrange("p n t -> p (n t)").bitcast(I32))
-            return w
+        load_scales("hn", Whn_s)
+        load_scales("in", Win_s)
+        load_scales("iz", Wiz_s)
+        load_scales("hz", Whz_s)
 
         def quantise(src, nm, banks, copy):
             words = src[:].bitcast(F32)
@@ -126,17 +103,10 @@ def tile_gru_w_kernel(
         nc.vector.quantize_mx(out=xc[:].bitcast(FP8X4), scales=xs[:], in_=xg[:])
         nc.vector.quantize_mx(out=hc[:].bitcast(FP8X4), scales=hs[:], in_=hg[:])
 
-        bias = {}
-        for q, nm in ((0, "r"), (1, "hn"), (2, "in"), (3, "z")):
-            bt = keep.tile([P, H], F32, name="bias_" + nm)
-            for j in range(4):
-                pb = bank(4 + j, [P, NT])
-                nc.tensor.matmul(pb[:], lhsT=sel[:, q, :], rhs=brow[:, cols(j)], start=True, stop=True)
-                if j % 2 == 0:
-                    nc.scalar.copy(out=bt[:, cols(j)], in_=pb[:])
-                else:
-                    nc.vector.tensor_copy(out=bt[:, cols(j)], in_=pb[:])
-            bias[nm] = bt
+        def load_full(words, g):
+            w = wpool.tile([P, H], U32, name="w", tag="w", align_bytes=64)
+            nc.sync.dma_start(out=w[:].bitcast(I32), in_=words[g].rearrange("p n t -> p (n t)").bitcast(I32))
+            return w
 
         def mx(acc, cd, sc, g, w_ap, s_ap, start, stop):
             nc.tensor.matmul_mx(
@@ -149,56 +119,76 @@ def tile_gru_w_kernel(
                 stop=stop,
             )
 
-        def full_phase(accs, parts):
-            n = len(parts)
-            for i, (nm, s, words, cd, sc) in enumerate(parts):
-                for g in range(G):
-                    w = load_full(nm, s, words, g)
-                    for j in range(4):
-                        mx(accs[j][:], cd, sc, g, w[:, cols(j)], planes[nm][4 * g:P, cols(j)],
-                           i == 0 and g == 0, i == n - 1 and g == G - 1)
+        def weight_phase(accs, nm, words, cd, sc, first, last):
+            for g in range(G):
+                w = load_full(words, g)
+                for j in range(4):
+                    mx(accs[j][:], cd, sc, g, w[:, cols(j)], planes[nm][4 * g:P, cols(j)],
+                       first and g == 0, last and g == G - 1)
 
-        r_t = keep.tile([P, H], F32, name="r_t")
         acc = [bank(j, [P, NT]) for j in range(4)]
-        full_phase(acc, (("ir", Wir_s, Wir_w, xc, xs), ("hr", Whr_s, Whr_w, hc, hs)))
+        weight_phase(acc, "ir", Wir_w, xc, xs, True, False)
+
+        bias = {}
+        for q, nm in ((0, "r"), (1, "hn"), (2, "in"), (3, "z")):
+            bt = keep.tile([P, H], F32, name="bias_" + nm)
+            for j in range(4):
+                pb = bank(4 + j, [P, NT])
+                nc.tensor.matmul(pb[:], lhsT=sel[:, q, :], rhs=brow[:, cols(j)], start=True, stop=True)
+                if j % 2 == 0:
+                    nc.scalar.copy(out=bt[:, cols(j)], in_=pb[:])
+                else:
+                    nc.vector.tensor_copy(out=bt[:, cols(j)], in_=pb[:])
+            bias[nm] = bt
+
+        weight_phase(acc, "hr", Whr_w, hc, hs, False, True)
+        r_t = keep.tile([P, H], F32, name="r_t")
         for j in range(4):
             nc.vector.tensor_tensor(out=r_t[:, cols(j)], in0=acc[j][:], in1=bias["r"][:, cols(j)], op=ADD)
             nc.scalar.activation(out=r_t[:, cols(j)], in_=r_t[:, cols(j)], func=ACT.Sigmoid)
 
         c_t = keep.tile([P, H], F32, name="c_t")
         acc = [bank(4 + j, [P, NT]) for j in range(4)]
-        full_phase(acc, (("hn", Whn_s, Whn_w, hc, hs),))
+        weight_phase(acc, "hn", Whn_w, hc, hs, True, True)
         for j in range(4):
             cs = cols(j)
             nc.vector.tensor_tensor(out=c_t[:, cs], in0=acc[j][:], in1=bias["hn"][:, cs], op=ADD)
+        for j in range(4):
+            cs = cols(j)
             nc.vector.tensor_tensor(out=c_t[:, cs], in0=c_t[:, cs], in1=r_t[:, cs], op=MUL)
+        for j in range(4):
+            cs = cols(j)
             nc.vector.tensor_tensor(out=c_t[:, cs], in0=c_t[:, cs], in1=bias["in"][:, cs], op=ADD)
 
         n_t = keep.tile([P, H], F32, name="n_t")
-        d_t = keep.tile([P, H], F32, name="d_t")
+        d_t = r_t
         acc = [bank(j, [P, NT]) for j in range(4)]
-        full_phase(acc, (("in", Win_s, Win_w, xc, xs),))
+        weight_phase(acc, "in", Win_w, xc, xs, True, True)
         for j in range(4):
             cs = cols(j)
             nc.vector.tensor_tensor(out=n_t[:, cs], in0=acc[j][:], in1=c_t[:, cs], op=ADD)
             nc.scalar.activation(out=n_t[:, cs], in_=n_t[:, cs], func=ACT.Tanh)
+        nc.scalar.activation(out=warm[:, 1:2], in_=warm[:, 0:1], func=ACT.Sigmoid)
+        for j in range(4):
+            cs = cols(j)
             nc.vector.tensor_tensor(out=d_t[:, cs], in0=h_sb[:, cs], in1=n_t[:, cs], op=SUB)
 
         z_t = keep.tile([P, H], F32, name="z_t")
         accz = [bank(ZBANK[c], [P, wd]) for c, (c0, wd) in enumerate(ZCH)]
         for g in range(G):
-            w = load_full("iz", Wiz_s, Wiz_w, g)
+            w = load_full(Wiz_w, g)
             for c, (c0, wd) in enumerate(ZCH):
                 mx(accz[c][:], xc, xs, g, w[:, c0:c0 + wd], planes["iz"][4 * g:P, c0:c0 + wd], g == 0, False)
-        if SCALE_MODE == "woven":
-            load_scales("hz", Whz_s)
+        wzs = []
         for c, (c0, wd) in enumerate(ZCH):
-            cs = slice(c0, c0 + wd)
             wz = wpool.tile([P, G, wd], U32, name="w", tag="w", align_bytes=64)
             nc.sync.dma_start(out=wz[:].bitcast(I32),
-                              in_=Whz_w[:, :, cs, :].rearrange("g p n t -> p g (n t)").bitcast(I32))
+                              in_=Whz_w[:, :, c0:c0 + wd, :].rearrange("g p n t -> p g (n t)").bitcast(I32))
+            wzs.append(wz)
+        for c, (c0, wd) in enumerate(ZCH):
+            cs = slice(c0, c0 + wd)
             for g in range(G):
-                mx(accz[c][:], hc, hs, g, wz[:, g, :], planes["hz"][4 * g:P, cs], False, g == G - 1)
+                mx(accz[c][:], hc, hs, g, wzs[c][:, g, :], planes["hz"][4 * g:P, cs], False, g == G - 1)
             nc.vector.tensor_tensor(out=z_t[:, cs], in0=accz[c][:], in1=bias["z"][:, cs], op=ADD)
             nc.scalar.activation(out=z_t[:, cs], in_=z_t[:, cs], func=ACT.Sigmoid)
             nc.vector.tensor_tensor(out=z_t[:, cs], in0=z_t[:, cs], in1=d_t[:, cs], op=MUL)

@@ -74,7 +74,9 @@ def tile_gru_w_kernel(
                 nc.gpsimd.dma_start(out=planes[nm][32 * q:32 * q + 16, :].bitcast(F32),
                                     in_=s[:, 4 * q:4 * q + 4, :].bitcast(F32))
 
-        load_scales("ir", Wir_s)
+        for q in range(4):
+            nc.sync.dma_start(out=planes["ir"][32 * q:32 * q + 16, :].bitcast(I32),
+                              in_=Wir_s[:, 4 * q:4 * q + 4, :].bitcast(I32))
         load_scales("hr", Whr_s)
         for row, b in ((0, Wir_b), (1, Whr_b), (32, Whn_b), (64, Win_b), (96, Wiz_b), (97, Whz_b)):
             nc.gpsimd.dma_start(out=brow[row:row + 1, :], in_=b.unsqueeze(0))
@@ -185,12 +187,38 @@ def tile_gru_w_kernel(
             nc.sync.dma_start(out=wz[:].bitcast(I32),
                               in_=Whz_w[:, :, c0:c0 + wd, :].rearrange("g p n t -> p g (n t)").bitcast(I32))
             wzs.append(wz)
-        for c, (c0, wd) in enumerate(ZCH):
-            cs = slice(c0, c0 + wd)
+        def passes(c):
+            c0, wd = ZCH[c]
             for g in range(G):
-                mx(accz[c][:], hc, hs, g, wzs[c][:, g, :], planes["hz"][4 * g:P, cs], False, g == G - 1)
-            nc.vector.tensor_tensor(out=z_t[:, cs], in0=accz[c][:], in1=bias["z"][:, cs], op=ADD)
+                mx(accz[c][:], hc, hs, g, wzs[c][:, g, :], planes["hz"][4 * g:P, c0:c0 + wd], False, g == G - 1)
+
+        def gate(c, o, wd):
+            cs = slice(ZCH[c][0] + o, ZCH[c][0] + o + wd)
+            nc.vector.tensor_tensor(out=z_t[:, cs], in0=accz[c][:, o:o + wd], in1=bias["z"][:, cs], op=ADD)
             nc.scalar.activation(out=z_t[:, cs], in_=z_t[:, cs], func=ACT.Sigmoid)
+
+        def blend(c, o, wd):
+            cs = slice(ZCH[c][0] + o, ZCH[c][0] + o + wd)
             nc.vector.tensor_tensor(out=z_t[:, cs], in0=z_t[:, cs], in1=d_t[:, cs], op=MUL)
             nc.vector.tensor_tensor(out=z_t[:, cs], in0=z_t[:, cs], in1=n_t[:, cs], op=ADD)
-            nc.sync.dma_start(out=out[:, cs], in_=z_t[:, cs])
+
+        def store(c):
+            c0, wd = ZCH[c]
+            nc.sync.dma_start(out=out[:, c0:c0 + wd], in_=z_t[:, c0:c0 + wd])
+
+        for c in range(3):
+            passes(c)
+            for o in (0, 256):
+                gate(c, o, 256)
+            for o in (0, 256):
+                blend(c, o, 256)
+            store(c)
+        passes(3)
+        gate(3, 0, 256)
+        for c in (4, 5):
+            passes(c)
+            gate(c, 0, 128)
+            blend(c - 1, 0, ZCH[c - 1][1])
+            store(c - 1)
+        blend(5, 0, 128)
+        store(5)

@@ -78,8 +78,6 @@ def tile_gru_w_kernel(
             nc.sync.dma_start(out=planes["ir"][32 * q:32 * q + 16, :].bitcast(I32),
                               in_=Wir_s[:, 4 * q:4 * q + 4, :].bitcast(I32))
         load_scales("hr", Whr_s)
-        for row, b in ((0, Wir_b), (1, Whr_b), (32, Whn_b), (64, Win_b), (96, Wiz_b), (97, Whz_b)):
-            nc.gpsimd.dma_start(out=brow[row:row + 1, :], in_=b.unsqueeze(0))
         load_scales("hn", Whn_s)
         load_scales("in", Win_s)
         load_scales("iz", Wiz_s)
@@ -131,6 +129,8 @@ def tile_gru_w_kernel(
         acc = [bank(j, [P, NT]) for j in range(4)]
         weight_phase(acc, "ir", Wir_w, xc, xs, True, False)
 
+        for row, b in ((0, Wir_b), (1, Whr_b), (32, Whn_b), (64, Win_b), (96, Wiz_b), (97, Whz_b)):
+            nc.scalar.dma_start(out=brow[row:row + 1, :], in_=b.unsqueeze(0))
         bias = {}
         for q, nm in ((0, "r"), (1, "hn"), (2, "in"), (3, "z")):
             bt = keep.tile([P, H], F32, name="bias_" + nm)

@@ -21,8 +21,8 @@ NT = 512
 FLOPS = 2 * 128 * 2048 * 2048 * 6
 
 NW = 14
-ZCH = ((0, 512), (512, 512), (1024, 512), (1536, 256), (1792, 128), (1920, 128))
-ZBANK = (4, 5, 6, 7, 0, 1)
+ZCH = ((0, 256), (256, 256), (512, 512), (1024, 256), (1280, 256), (1536, 256), (1792, 256))
+ZBANK = (4, 5, 6, 7, 0, 1, 2)
 
 
 def tile_gru_w_kernel(
@@ -192,33 +192,29 @@ def tile_gru_w_kernel(
             for g in range(G):
                 mx(accz[c][:], hc, hs, g, wzs[c][:, g, :], planes["hz"][4 * g:P, c0:c0 + wd], False, g == G - 1)
 
-        def gate(c, o, wd):
-            cs = slice(ZCH[c][0] + o, ZCH[c][0] + o + wd)
-            nc.vector.tensor_tensor(out=z_t[:, cs], in0=accz[c][:, o:o + wd], in1=bias["z"][:, cs], op=ADD)
-            nc.scalar.activation(out=z_t[:, cs], in_=z_t[:, cs], func=ACT.Sigmoid)
-
-        def blend(c, o, wd):
-            cs = slice(ZCH[c][0] + o, ZCH[c][0] + o + wd)
-            nc.vector.tensor_tensor(out=z_t[:, cs], in0=z_t[:, cs], in1=d_t[:, cs], op=MUL)
-            nc.vector.tensor_tensor(out=z_t[:, cs], in0=z_t[:, cs], in1=n_t[:, cs], op=ADD)
-
-        def store(c):
+        def gate(c):
             c0, wd = ZCH[c]
-            nc.sync.dma_start(out=out[:, c0:c0 + wd], in_=z_t[:, c0:c0 + wd])
+            for o in range(0, wd, 256):
+                cs = slice(c0 + o, c0 + o + 256)
+                nc.vector.tensor_tensor(out=z_t[:, cs], in0=accz[c][:, o:o + 256], in1=bias["z"][:, cs], op=ADD)
+                nc.scalar.activation(out=z_t[:, cs], in_=z_t[:, cs], func=ACT.Sigmoid)
 
-        for c in range(3):
+        def times_d(c):
+            cs = slice(ZCH[c][0], ZCH[c][0] + ZCH[c][1])
+            nc.vector.tensor_tensor(out=z_t[:, cs], in0=z_t[:, cs], in1=d_t[:, cs], op=MUL)
+
+        def plus_n(c):
+            cs = slice(ZCH[c][0], ZCH[c][0] + ZCH[c][1])
+            nc.vector.tensor_tensor(out=z_t[:, cs], in0=z_t[:, cs], in1=n_t[:, cs], op=ADD)
+            nc.sync.dma_start(out=out[:, cs], in_=z_t[:, cs])
+
+        for c in range(len(ZCH)):
             passes(c)
-            for o in (0, 256):
-                gate(c, o, 256)
-            for o in (0, 256):
-                blend(c, o, 256)
-            store(c)
-        passes(3)
-        gate(3, 0, 256)
-        for c in (4, 5):
-            passes(c)
-            gate(c, 0, 128)
-            blend(c - 1, 0, ZCH[c - 1][1])
-            store(c - 1)
-        blend(5, 0, 128)
-        store(5)
+            gate(c)
+            if c > 0:
+                times_d(c - 1)
+            if c > 1:
+                plus_n(c - 2)
+        times_d(len(ZCH) - 1)
+        plus_n(len(ZCH) - 2)
+        plus_n(len(ZCH) - 1)

@@ -20,7 +20,7 @@ G = 4
 NT = 512
 FLOPS = 2 * 128 * 2048 * 2048 * 6
 
-NW = 14
+NW = 4
 ZCH = ((0, 256), (256, 256), (512, 512), (1024, 256), (1280, 256), (1536, 256), (1792, 256))
 ZBANK = (4, 5, 6, 7, 0, 1, 2)
 
@@ -103,10 +103,12 @@ def tile_gru_w_kernel(
         nc.vector.quantize_mx(out=xc[:].bitcast(FP8X4), scales=xs[:], in_=xg[:])
         nc.vector.quantize_mx(out=hc[:].bitcast(FP8X4), scales=hs[:], in_=hg[:])
 
-        def load_full(words, g):
-            w = wpool.tile([P, H], U32, name="w", tag="w", align_bytes=64)
-            nc.sync.dma_start(out=w[:].bitcast(I32), in_=words[g].rearrange("p n t -> p (n t)").bitcast(I32))
-            return w
+        def load_part(w, words, g0, g1, c0, wd):
+            nc.sync.dma_start(out=w[:, g0:g1, c0:c0 + wd].bitcast(I32),
+                              in_=words[g0:g1, :, c0:c0 + wd, :].rearrange("g p n t -> p g (n t)").bitcast(I32))
+
+        def weight_tile():
+            return wpool.tile([P, G, H], U32, name="w", tag="w", align_bytes=64)
 
         def mx(acc, cd, sc, g, w_ap, s_ap, start, stop):
             nc.tensor.matmul_mx(
@@ -120,10 +122,11 @@ def tile_gru_w_kernel(
             )
 
         def weight_phase(accs, nm, words, cd, sc, first, last):
+            w = weight_tile()
+            load_part(w, words, 0, G, 0, H)
             for g in range(G):
-                w = load_full(words, g)
                 for j in range(4):
-                    mx(accs[j][:], cd, sc, g, w[:, cols(j)], planes[nm][4 * g:P, cols(j)],
+                    mx(accs[j][:], cd, sc, g, w[:, g, cols(j)], planes[nm][4 * g:P, cols(j)],
                        first and g == 0, last and g == G - 1)
 
         acc = [bank(j, [P, NT]) for j in range(4)]
@@ -177,20 +180,20 @@ def tile_gru_w_kernel(
 
         z_t = keep.tile([P, H], F32, name="z_t")
         accz = [bank(ZBANK[c], [P, wd]) for c, (c0, wd) in enumerate(ZCH)]
+        w = weight_tile()
+        load_part(w, Wiz_w, 0, 2, 0, H)
+        load_part(w, Wiz_w, 2, 4, 0, H)
         for g in range(G):
-            w = load_full(Wiz_w, g)
             for c, (c0, wd) in enumerate(ZCH):
-                mx(accz[c][:], xc, xs, g, w[:, c0:c0 + wd], planes["iz"][4 * g:P, c0:c0 + wd], g == 0, False)
-        wzs = []
-        for c, (c0, wd) in enumerate(ZCH):
-            wz = wpool.tile([P, G, wd], U32, name="w", tag="w", align_bytes=64)
-            nc.sync.dma_start(out=wz[:].bitcast(I32),
-                              in_=Whz_w[:, :, c0:c0 + wd, :].rearrange("g p n t -> p g (n t)").bitcast(I32))
-            wzs.append(wz)
+                mx(accz[c][:], xc, xs, g, w[:, g, c0:c0 + wd], planes["iz"][4 * g:P, c0:c0 + wd], g == 0, False)
+        wz = weight_tile()
+        for c0, wd in ZCH:
+            load_part(wz, Whz_w, 0, G, c0, wd)
+
         def passes(c):
             c0, wd = ZCH[c]
             for g in range(G):
-                mx(accz[c][:], hc, hs, g, wzs[c][:, g, :], planes["hz"][4 * g:P, c0:c0 + wd], False, g == G - 1)
+                mx(accz[c][:], hc, hs, g, wz[:, g, c0:c0 + wd], planes["hz"][4 * g:P, c0:c0 + wd], False, g == G - 1)
 
         def gate(c):
             c0, wd = ZCH[c]

@@ -21,8 +21,8 @@ NT = 512
 FLOPS = 2 * 128 * 2048 * 2048 * 6
 
 NW = 4
-ZCH = ((0, 256), (256, 256), (512, 512), (1024, 256), (1280, 256), (1536, 256), (1792, 256))
-ZBANK = (4, 5, 6, 7, 0, 1, 2)
+ZCH = ((0, 256), (256, 512), (768, 256), (1024, 256), (1280, 256), (1536, 256), (1792, 128), (1920, 128))
+ZBANK = (4, 5, 6, 7, 0, 1, 2, 3)
 
 
 def tile_gru_w_kernel(
@@ -121,9 +121,10 @@ def tile_gru_w_kernel(
                 stop=stop,
             )
 
-        def weight_phase(accs, nm, words, cd, sc, first, last):
+        def weight_phase(accs, nm, words, cd, sc, first, last, loads=1):
             w = weight_tile()
-            load_part(w, words, 0, G, 0, H)
+            for g in range(0, G, G // loads):
+                load_part(w, words, g, g + G // loads, 0, H)
             for g in range(G):
                 for j in range(4):
                     mx(accs[j][:], cd, sc, g, w[:, g, cols(j)], planes[nm][4 * g:P, cols(j)],
@@ -168,7 +169,7 @@ def tile_gru_w_kernel(
         n_t = keep.tile([P, H], F32, name="n_t")
         d_t = r_t
         acc = [bank(j, [P, NT]) for j in range(4)]
-        weight_phase(acc, "in", Win_w, xc, xs, True, True)
+        weight_phase(acc, "in", Win_w, xc, xs, True, True, loads=2)
         for j in range(4):
             cs = cols(j)
             nc.vector.tensor_tensor(out=n_t[:, cs], in0=acc[j][:], in1=c_t[:, cs], op=ADD)
@@ -188,7 +189,11 @@ def tile_gru_w_kernel(
                 mx(accz[c][:], xc, xs, g, w[:, g, c0:c0 + wd], planes["iz"][4 * g:P, c0:c0 + wd], g == 0, False)
         wz = weight_tile()
         for c0, wd in ZCH:
-            load_part(wz, Whz_w, 0, G, c0, wd)
+            if wd > 256:
+                load_part(wz, Whz_w, 0, G - 1, c0, wd)
+                load_part(wz, Whz_w, G - 1, G, c0, wd)
+            else:
+                load_part(wz, Whz_w, 0, G, c0, wd)
 
         def passes(c):
             c0, wd = ZCH[c]
@@ -198,8 +203,9 @@ def tile_gru_w_kernel(
         def gate(c):
             c0, wd = ZCH[c]
             for o in range(0, wd, 256):
-                cs = slice(c0 + o, c0 + o + 256)
-                nc.vector.tensor_tensor(out=z_t[:, cs], in0=accz[c][:, o:o + 256], in1=bias["z"][:, cs], op=ADD)
+                n = min(256, wd - o)
+                cs = slice(c0 + o, c0 + o + n)
+                nc.vector.tensor_tensor(out=z_t[:, cs], in0=accz[c][:, o:o + n], in1=bias["z"][:, cs], op=ADD)
                 nc.scalar.activation(out=z_t[:, cs], in_=z_t[:, cs], func=ACT.Sigmoid)
 
         def times_d(c):

from contextlib import ExitStack

import concourse.mybir as mybir
from concourse.masks import make_identity

F32 = mybir.dt.float32
BF16 = mybir.dt.bfloat16
I32 = mybir.dt.int32
U32 = mybir.dt.uint32
U8 = mybir.dt.uint8
FP8X4 = mybir.dt.float8_e4m3fn_x4
ADD = mybir.AluOpType.add
SUB = mybir.AluOpType.subtract
MUL = mybir.AluOpType.mult
ACT = mybir.ActivationFunctionType

P = 128
H = 2048
G = 4
NT = 512
FLOPS = 2 * 128 * 2048 * 2048 * 6

NW = 4
ZCH = ((0, 256), (256, 512), (768, 256), (1024, 256), (1280, 256), (1536, 256), (1792, 128), (1920, 128))
ZBANK = (4, 5, 6, 7, 0, 1, 2, 3)


def tile_gru_w_kernel(
    tc, x, hidden,
    Wir_w, Wir_s, Wir_b, Whr_w, Whr_s, Whr_b,
    Wiz_w, Wiz_s, Wiz_b, Whz_w, Whz_s, Whz_b,
    Win_w, Win_s, Win_b, Whn_w, Whn_s, Whn_b,
    out,
):
    nc = tc.nc
    with ExitStack() as ctx:
        keep = ctx.enter_context(tc.tile_pool(name="keep", bufs=1))
        wpool = ctx.enter_context(tc.tile_pool(name="wpool", bufs=NW))
        psum = ctx.enter_context(tc.psum_pool(name="psum", bufs=1))
        ctx.enter_context(tc.manual_schedule())

        def bank(i, shape):
            return psum.tile(shape, F32, name="bk%d" % i, tag="bk%d" % i)

        def cols(j):
            return slice(NT * j, NT * (j + 1))

        x_sb = keep.tile([P, H], BF16, name="x_sb")
        h_sb = keep.tile([P, H], BF16, name="h_sb")
        nc.sync.dma_start(out=x_sb[:], in_=x)
        nc.sync.dma_start(out=h_sb[:], in_=hidden)

        ident = keep.tile([P, P], F32, name="ident")
        make_identity(nc, ident[:])
        warm = keep.tile([P, 2], F32, name="warm")
        planes = {}
        for nm in ("ir", "hr"):
            planes[nm] = keep.tile([P, H], U8, name="pl_" + nm, align_bytes=64)
            nc.vector.memset(planes[nm][:].bitcast(I32), 0)
        nc.vector.memset(warm[:], 0.0)
        nc.scalar.activation(out=warm[:, 1:2], in_=warm[:, 0:1], func=ACT.Sigmoid)
        brow = keep.tile([P, H], BF16, name="brow")
        nc.vector.memset(brow[:].bitcast(I32), 0)
        sel = keep.tile([P, 4, P], BF16, name="sel")
        nc.vector.memset(sel[:].rearrange("p q m -> p (q m)").bitcast(I32), 0)
        for q in range(4):
            nc.vector.memset(sel[32 * q:32 * q + 32, q, :], 1.0)
        for nm in ("hn", "in", "iz", "hz"):
            planes[nm] = keep.tile([P, H], U8, name="pl_" + nm, align_bytes=64)
            nc.vector.memset(planes[nm][:].bitcast(I32), 0)

        def load_scales(nm, s):
            for q in range(4):
                nc.gpsimd.dma_start(out=planes[nm][32 * q:32 * q + 16, :].bitcast(F32),
                                    in_=s[:, 4 * q:4 * q + 4, :].bitcast(F32))

        for q in range(4):
            nc.sync.dma_start(out=planes["ir"][32 * q:32 * q + 16, :].bitcast(I32),
                              in_=Wir_s[:, 4 * q:4 * q + 4, :].bitcast(I32))
        load_scales("hr", Whr_s)
        load_scales("hn", Whn_s)
        load_scales("in", Win_s)
        load_scales("iz", Wiz_s)
        load_scales("hz", Whz_s)

        def quantise(src, nm, banks, copy):
            words = src[:].bitcast(F32)
            grouped = keep.tile([P, H], BF16, name="grp_" + nm, align_bytes=64)
            codes = keep.tile([P, G * P], U32, name="cod_" + nm, align_bytes=64)
            scl = keep.tile([P, G * P], U8, name="scl_" + nm, align_bytes=64)
            gview = grouped[:].bitcast(F32).rearrange("p (g b u) -> p g b u", g=G, u=2)
            for half in range(2):
                xt = bank(banks[half], [P, 4, P])
                for gl in range(2):
                    g = 2 * half + gl
                    for u in range(2):
                        nc.tensor.transpose(xt[:, 2 * gl + u, :], words[:, 256 * g + u:256 * (g + 1):2], ident[:])
                copy(out=gview[:, 2 * half:2 * half + 2, :, :], in_=xt[:].rearrange("p (gl u) b -> p gl b u", u=2))
            return grouped, codes, scl

        xg, xc, xs = quantise(x_sb, "x", (0, 1), nc.vector.tensor_copy)
        hg, hc, hs = quantise(h_sb, "h", (2, 3), nc.scalar.copy)
        nc.vector.quantize_mx(out=xc[:].bitcast(FP8X4), scales=xs[:], in_=xg[:])
        nc.vector.quantize_mx(out=hc[:].bitcast(FP8X4), scales=hs[:], in_=hg[:])

        def load_part(w, words, g0, g1, c0, wd):
            nc.sync.dma_start(out=w[:, g0:g1, c0:c0 + wd].bitcast(I32),
                              in_=words[g0:g1, :, c0:c0 + wd, :].rearrange("g p n t -> p g (n t)").bitcast(I32))

        def weight_tile():
            return wpool.tile([P, G, H], U32, name="w", tag="w", align_bytes=64)

        def mx(acc, cd, sc, g, w_ap, s_ap, start, stop):
            nc.tensor.matmul_mx(
                out=acc,
                lhsT=cd[:, P * g:P * (g + 1)].bitcast(FP8X4),
                lhsT_scale=sc[:, P * g:P * (g + 1)],
                rhs=w_ap.bitcast(FP8X4),
                rhs_scale=s_ap,
                start=start,
                stop=stop,
            )

        def weight_phase(accs, nm, words, cd, sc, first, last, loads=1):
            w = weight_tile()
            for g in range(0, G, G // loads):
                load_part(w, words, g, g + G // loads, 0, H)
            for g in range(G):
                for j in range(4):
                    mx(accs[j][:], cd, sc, g, w[:, g, cols(j)], planes[nm][4 * g:P, cols(j)],
                       first and g == 0, last and g == G - 1)

        acc = [bank(j, [P, NT]) for j in range(4)]
        weight_phase(acc, "ir", Wir_w, xc, xs, True, False)

        for row, b in ((0, Wir_b), (1, Whr_b), (32, Whn_b), (64, Win_b), (96, Wiz_b), (97, Whz_b)):
            nc.scalar.dma_start(out=brow[row:row + 1, :], in_=b.unsqueeze(0))
        bias = {}
        for q, nm in ((0, "r"), (1, "hn"), (2, "in"), (3, "z")):
            bt = keep.tile([P, H], F32, name="bias_" + nm)
            for j in range(4):
                pb = bank(4 + j, [P, NT])
                nc.tensor.matmul(pb[:], lhsT=sel[:, q, :], rhs=brow[:, cols(j)], start=True, stop=True)
                if j % 2 == 0:
                    nc.scalar.copy(out=bt[:, cols(j)], in_=pb[:])
                else:
                    nc.vector.tensor_copy(out=bt[:, cols(j)], in_=pb[:])
            bias[nm] = bt

        weight_phase(acc, "hr", Whr_w, hc, hs, False, True)
        r_t = keep.tile([P, H], F32, name="r_t")
        for j in range(4):
            nc.vector.tensor_tensor(out=r_t[:, cols(j)], in0=acc[j][:], in1=bias["r"][:, cols(j)], op=ADD)
            nc.scalar.activation(out=r_t[:, cols(j)], in_=r_t[:, cols(j)], func=ACT.Sigmoid)

        c_t = keep.tile([P, H], F32, name="c_t")
        acc = [bank(4 + j, [P, NT]) for j in range(4)]
        weight_phase(acc, "hn", Whn_w, hc, hs, True, True)
        for j in range(4):
            cs = cols(j)
            nc.vector.tensor_tensor(out=c_t[:, cs], in0=acc[j][:], in1=bias["hn"][:, cs], op=ADD)
        for j in range(4):
            cs = cols(j)
            nc.vector.tensor_tensor(out=c_t[:, cs], in0=c_t[:, cs], in1=r_t[:, cs], op=MUL)
        for j in range(4):
            cs = cols(j)
            nc.vector.tensor_tensor(out=c_t[:, cs], in0=c_t[:, cs], in1=bias["in"][:, cs], op=ADD)

        n_t = keep.tile([P, H], F32, name="n_t")
        d_t = r_t
        acc = [bank(j, [P, NT]) for j in range(4)]
        weight_phase(acc, "in", Win_w, xc, xs, True, True, loads=2)
        for j in range(4):
            cs = cols(j)
            nc.vector.tensor_tensor(out=n_t[:, cs], in0=acc[j][:], in1=c_t[:, cs], op=ADD)
            nc.scalar.activation(out=n_t[:, cs], in_=n_t[:, cs], func=ACT.Tanh)
        nc.scalar.activation(out=warm[:, 1:2], in_=warm[:, 0:1], func=ACT.Sigmoid)
        for j in range(4):
            cs = cols(j)
            nc.vector.tensor_tensor(out=d_t[:, cs], in0=h_sb[:, cs], in1=n_t[:, cs], op=SUB)

        z_t = keep.tile([P, H], F32, name="z_t")
        accz = [bank(ZBANK[c], [P, wd]) for c, (c0, wd) in enumerate(ZCH)]
        w = weight_tile()
        load_part(w, Wiz_w, 0, 2, 0, H)
        load_part(w, Wiz_w, 2, 4, 0, H)
        for g in range(G):
            for c, (c0, wd) in enumerate(ZCH):
                mx(accz[c][:], xc, xs, g, w[:, g, c0:c0 + wd], planes["iz"][4 * g:P, c0:c0 + wd], g == 0, False)
        wz = weight_tile()
        for c0, wd in ZCH:
            if wd > 256:
                load_part(wz, Whz_w, 0, G - 1, c0, wd)
                load_part(wz, Whz_w, G - 1, G, c0, wd)
            else:
                load_part(wz, Whz_w, 0, G, c0, wd)

        def passes(c):
            c0, wd = ZCH[c]
            for g in range(G):
                mx(accz[c][:], hc, hs, g, wz[:, g, c0:c0 + wd], planes["hz"][4 * g:P, c0:c0 + wd], False, g == G - 1)

        def gate(c):
            c0, wd = ZCH[c]
            for o in range(0, wd, 256):
                n = min(256, wd - o)
                cs = slice(c0 + o, c0 + o + n)
                nc.vector.tensor_tensor(out=z_t[:, cs], in0=accz[c][:, o:o + n], in1=bias["z"][:, cs], op=ADD)
                nc.scalar.activation(out=z_t[:, cs], in_=z_t[:, cs], func=ACT.Sigmoid)

        def times_d(c):
            cs = slice(ZCH[c][0], ZCH[c][0] + ZCH[c][1])
            nc.vector.tensor_tensor(out=z_t[:, cs], in0=z_t[:, cs], in1=d_t[:, cs], op=MUL)

        def plus_n(c):
            cs = slice(ZCH[c][0], ZCH[c][0] + ZCH[c][1])
            nc.vector.tensor_tensor(out=z_t[:, cs], in0=z_t[:, cs], in1=n_t[:, cs], op=ADD)
            nc.sync.dma_start(out=out[:, cs], in_=z_t[:, cs])

        for c in range(len(ZCH)):
            passes(c)
            gate(c)
            if c > 0:
                times_d(c - 1)
            if c > 1:
                plus_n(c - 2)
        times_d(len(ZCH) - 1)
        plus_n(len(ZCH) - 2)
        plus_n(len(ZCH) - 1)
